import numpy as np
import ml_dtypes


def mxq(x, axis, fmt="e4m3"):
    dtype, down = {"e4m3": (ml_dtypes.float8_e4m3fn, 7), "e5m2": (ml_dtypes.float8_e5m2, 14)}[fmt]
    v = np.moveaxis(np.asarray(x, np.float32).astype(ml_dtypes.bfloat16).astype(np.float64), axis, -1)
    blocks = v.reshape(v.shape[:-1] + (-1, 32))
    amax = np.abs(blocks).max(-1, keepdims=True)
    byte = np.maximum(np.where(amax > 0, np.frexp(amax)[1] - 1 + 127, 0) - down, 1)
    scale = np.exp2(byte - 127.0)
    codes = (blocks / scale).astype(np.float32).astype(dtype).astype(np.float64)
    return np.moveaxis((codes * scale).reshape(v.shape), -1, axis)


WIDE = False


def mx_kscale(k):
    if not WIDE:
        return np.ones(k)
    levels = np.array([10, -10, 5, -5, 0])
    if k % 512:
        return np.exp2(np.random.permutation(np.resize(levels, k // 32))).repeat(32)
    a = np.empty((k // 512, 16))
    for p in range(k // 512):
        a[p, :8] = np.random.permutation(np.resize(levels, 8))
        for g in range(8):
            far = levels[np.abs(levels - a[p, g]) >= 10]
            a[p, g + 8] = far[np.random.randint(len(far))]
    return np.exp2(a.ravel()).repeat(32)


BF16 = ml_dtypes.bfloat16


def bf(x):
    return np.asarray(x, np.float32).astype(BF16)


def f64(x):
    return np.asarray(x).astype(np.float64)


NB, C, O, CZ, DD, HH, WW, MG = 1, 8192, 512, 512, 2, 4, 16, 4
STRIDES = (2, 2, 2)


def setup_inputs():
    s = mx_kscale(C)
    sd, sh, sw = STRIDES
    return {"x": bf(np.random.standard_normal((NB, C, DD, HH, WW)) * s[None, :, None, None, None]),
            "z": bf(np.random.standard_normal((NB, CZ, sd * DD + MG, sh * HH + MG, sw * WW + MG))),
            "W": bf(np.random.standard_normal((O, C)) / np.sqrt(C) / s[None, :]),
            "b": bf(np.random.standard_normal(O) * 0.5)}


def reference(x, z, W, b):
    sd, sh, sw = STRIDES
    u = np.repeat(np.repeat(np.repeat(f64(x), sd, axis=2), sh, axis=3), sw, axis=4)
    n, c, d, h, w = u.shape
    y = mxq(f64(W), 1, "e4m3") @ mxq(u.reshape(n, c, d * h * w), 1, "e4m3")
    y = y.reshape(n, -1, d, h, w) + f64(b)[None, :, None, None, None]
    zf = f64(z)
    off = [(zf.shape[i] - y.shape[i]) // 2 for i in range(2, 5)]
    zc = zf[:, :,
            off[0]:off[0] + y.shape[2],
            off[1]:off[1] + y.shape[3],
            off[2]:off[2] + y.shape[4]]
    return np.concatenate([y, zc], axis=1)

@@ -1,0 +1,256 @@
+from contextlib import ExitStack
+
+import concourse.mybir as mybir
+from concourse.masks import make_identity
+
+F32 = mybir.dt.float32
+BF16 = mybir.dt.bfloat16
+U32 = mybir.dt.uint32
+U8 = mybir.dt.uint8
+FP8X4 = mybir.dt.float8_e4m3fn_x4
+IDENTITY = mybir.ActivationFunctionType.Identity
+
+P = 128
+PACK = 4
+K_PASS = P * PACK
+PAIR = 2
+BANK_WORDS = 512
+PSUM_BANKS = 8
+
+CHANNELS = 8192
+OUT_CHANNELS = 512
+Z_CHANNELS = 512
+DEPTH = 2
+HEIGHT = 4
+WIDTH = 16
+POSITIONS = DEPTH * HEIGHT * WIDTH
+UP = 2
+UP_PLANE = UP * HEIGHT * UP * WIDTH
+UP_POSITIONS = UP * DEPTH * UP_PLANE
+MARGIN = 2
+Z_HEIGHT = UP * HEIGHT + 2 * MARGIN
+Z_WIDTH = UP * WIDTH + 2 * MARGIN
+
+PASSES = CHANNELS // K_PASS
+O_TILES = OUT_CHANNELS // P
+Z_TILES = Z_CHANNELS // P
+N_MOVING = UP * POSITIONS
+GROUPS = UP * UP
+
+PIECE_PASSES = 4
+PIECE_K = PIECE_PASSES * K_PASS
+PIECES = PASSES // PIECE_PASSES
+PIECE_BANKS = PIECE_K // PAIR // BANK_WORDS
+BANK_PASSES = PIECE_PASSES // PIECE_BANKS
+RUN_PIECES = (PSUM_BANKS - GROUPS) // PIECE_BANKS
+CHUNKS = PIECES // RUN_PIECES
+ALL_CHUNKS = O_TILES * CHUNKS
+Z_O_TILE = 2
+
+FLOPS = 2 * OUT_CHANNELS * CHANNELS * UP_POSITIONS
+BYTES = (
+    2 * (CHANNELS * POSITIONS + OUT_CHANNELS * CHANNELS + OUT_CHANNELS + Z_CHANNELS * UP_POSITIONS)
+    + 4 * (OUT_CHANNELS + Z_CHANNELS) * UP_POSITIONS
+)
+
+
+def tile_upconvcropcat_k_kernel(tc, x, z, W, b, out):
+    nc = tc.nc
+    x_rows = x.rearrange("n c d h w -> (n c) (d h w)")
+    z_rows = z.rearrange("n c d h w -> (n c) d (h w)")
+    out_rows = out.rearrange("n c d h w -> (n c) (d h w)")
+
+    with ExitStack() as stack:
+        const = stack.enter_context(tc.tile_pool(name="const", bufs=1))
+        x_raw_pool = stack.enter_context(tc.tile_pool(name="x_raw", bufs=PIECES))
+        w_raw_pool = stack.enter_context(tc.tile_pool(name="w_raw", bufs=O_TILES * PIECES))
+        z_raw_pool = stack.enter_context(tc.tile_pool(name="z_raw", bufs=Z_TILES))
+        x_mx_pool = stack.enter_context(tc.tile_pool(name="x_mx", bufs=PIECES))
+        stage = stack.enter_context(tc.tile_pool(name="stage", bufs=3 * RUN_PIECES))
+        results = stack.enter_context(tc.tile_pool(name="results", bufs=4))
+        acc_pool = stack.enter_context(tc.psum_pool(name="acc", bufs=GROUPS))
+        turned_pool = stack.enter_context(tc.psum_pool(name="turned", bufs=PSUM_BANKS - GROUPS))
+        stack.enter_context(tc.manual_schedule())
+
+        x_raws = []
+        w_raws = []
+        z_raws = []
+
+        def load_w_chunk(q):
+            m, n = divmod(q, CHUNKS)
+            for piece in range(n * RUN_PIECES, (n + 1) * RUN_PIECES):
+                w_raw = w_raw_pool.tile([P, PIECE_K], BF16)
+                nc.sync.dma_start(out=w_raw[:], in_=W[m * P : (m + 1) * P, piece * PIECE_K : (piece + 1) * PIECE_K])
+                w_raws.append(w_raw)
+
+        def load_x_chunk(n):
+            for piece in range(n * RUN_PIECES, (n + 1) * RUN_PIECES):
+                x_raw = x_raw_pool.tile([P, PIECE_K], BF16)
+                nc.sync.dma_start(
+                    out=x_raw[:].rearrange("p (g f) -> p g f", f=PACK * POSITIONS),
+                    in_=x_rows[piece * PIECE_K : (piece + 1) * PIECE_K, :].rearrange(
+                        "(g q t) w -> q g (t w)", q=P, t=PACK
+                    ),
+                )
+                x_raws.append(x_raw)
+
+        def load_z(i):
+            z_raw = z_raw_pool.tile([P, UP * DEPTH * Z_HEIGHT * Z_WIDTH], BF16)
+            nc.sync.dma_start(
+                out=z_raw[:],
+                in_=z_rows[i * P : (i + 1) * P, MARGIN : MARGIN + UP * DEPTH, :].rearrange("c d f -> c (d f)"),
+            )
+            z_raws.append(z_raw)
+
+        load_w_chunk(0)
+        load_w_chunk(1)
+        for q in range(ALL_CHUNKS - 2):
+            if q < CHUNKS:
+                load_x_chunk(q)
+            if q + 2 == (O_TILES - 1) * CHUNKS:
+                for i in range(Z_TILES):
+                    load_z(i)
+            load_w_chunk(q + 2)
+
+        identity = const.tile([P, P], F32)
+        make_identity(nc, identity[:])
+
+        def transpose_chunk(q):
+            banks = []
+            for w_raw in w_raws[q * RUN_PIECES : (q + 1) * RUN_PIECES]:
+                raw_words = w_raw[:].bitcast(F32)
+                for h in range(PIECE_BANKS):
+                    turned = turned_pool.tile([P, BANK_WORDS], F32, tag="turned")
+                    for s in range(BANK_WORDS // P):
+                        g, u = divmod(s, PAIR)
+                        first = h * BANK_WORDS + g * PAIR * P
+                        nc.tensor.transpose(
+                            out=turned[:, s * P : (s + 1) * P],
+                            in_=raw_words[:, first + u : first + PAIR * P : PAIR],
+                            identity=identity[:],
+                        )
+                    banks.append(turned)
+            return banks
+
+        def quantise_chunk(banks):
+            grouped = []
+            for i in range(RUN_PIECES):
+                w_grouped = stage.tile([P, PIECE_K], BF16, align_bytes=64)
+                grouped_words = w_grouped[:].bitcast(F32)
+                for h in range(PIECE_BANKS):
+                    copy = nc.scalar.copy if h == 0 else nc.vector.tensor_copy
+                    copy(
+                        out=grouped_words[:, h * BANK_WORDS : (h + 1) * BANK_WORDS].rearrange(
+                            "p (g o u) -> p g o u", g=BANK_PASSES, u=PAIR
+                        ),
+                        in_=banks[i * PIECE_BANKS + h][:].rearrange("p (g u o) -> p g o u", g=BANK_PASSES, u=PAIR),
+                    )
+                grouped.append(w_grouped)
+            quantised = []
+            for w_grouped in grouped:
+                w_words = stage.tile([P, PIECE_PASSES * P], U32, align_bytes=64)
+                w_scales = stage.tile([P, PIECE_PASSES * P], U8, align_bytes=64)
+                nc.vector.quantize_mx(out=w_words[:].bitcast(FP8X4), scales=w_scales[:], in_=w_grouped[:])
+                quantised.append((w_words, w_scales))
+            return quantised
+
+        x_quantised = []
+
+        def prepare_x(piece):
+            x_grouped = stage.tile([P, PIECE_K], BF16, align_bytes=64)
+            for g in range(PIECE_PASSES):
+                cols = slice(g * K_PASS, (g + 1) * K_PASS)
+                copy = nc.vector.tensor_copy if g % 2 == 0 else nc.scalar.copy
+                copy(
+                    out=x_grouped[:, cols].rearrange("p (c i t) -> p c t i", i=4, t=PACK),
+                    in_=x_raws[piece][:, cols].rearrange("p (t c i) -> p c t i", t=PACK, i=4),
+                )
+            x_words = x_mx_pool.tile([P, PIECE_PASSES * N_MOVING], U32, align_bytes=64)
+            x_scales = x_mx_pool.tile([P, PIECE_PASSES * N_MOVING], U8, align_bytes=64)
+            for g in range(PIECE_PASSES):
+                for r in range(UP):
+                    cols = slice(g * N_MOVING + r * POSITIONS, g * N_MOVING + (r + 1) * POSITIONS)
+                    nc.vector.quantize_mx(
+                        out=x_words[:, cols].bitcast(FP8X4),
+                        scales=x_scales[:, cols],
+                        in_=x_grouped[:, g * K_PASS : (g + 1) * K_PASS],
+                    )
+            x_quantised.append((x_words, x_scales))
+
+        def multiply(n, quantised, acc):
+            for i in range(RUN_PIECES):
+                w_words, w_scales = quantised[i]
+                x_words, x_scales = x_quantised[n * RUN_PIECES + i]
+                for g in range(PIECE_PASSES):
+                    c = (n * RUN_PIECES + i) * PIECE_PASSES + g
+                    o_cols = slice(g * P, (g + 1) * P)
+                    x_cols = slice(g * N_MOVING, (g + 1) * N_MOVING)
+                    for group in acc:
+                        nc.tensor.matmul_mx(
+                            out=group[:],
+                            lhsT=w_words[:, o_cols].bitcast(FP8X4),
+                            lhsT_scale=w_scales[:, o_cols],
+                            rhs=x_words[:, x_cols].bitcast(FP8X4),
+                            rhs_scale=x_scales[:, x_cols],
+                            start=(c == 0),
+                            stop=(c == PASSES - 1),
+                        )
+
+        def finish(m, acc):
+            planes = out_rows[m * P : (m + 1) * P, :].rearrange("o (i a f) -> o a i f", i=DEPTH, a=UP)
+            for a in range(UP):
+                y = results.tile([P, DEPTH * UP_PLANE], F32)
+                y_view = y[:].rearrange("p (i h b k r) -> p b i h k r", i=DEPTH, h=HEIGHT, b=UP, k=WIDTH, r=UP)
+                for bb in range(UP):
+                    sums = acc[a * UP + bb][:].rearrange("p (r i h k) -> p i h k r", r=UP, i=DEPTH, h=HEIGHT)
+                    if bb == 0:
+                        nc.scalar.activation(out=y_view[:, bb], in_=sums, func=IDENTITY, bias=bias[:, m : m + 1])
+                    else:
+                        nc.vector.tensor_scalar_add(out=y_view[:, bb], in0=sums, scalar1=bias[:, m : m + 1])
+                nc.sync.dma_start(out=planes[:, a], in_=y[:].rearrange("p (i f) -> p i f", i=DEPTH))
+
+        def crop_z(i):
+            cropped = results.tile([P, UP_POSITIONS], F32)
+            nc.vector.tensor_copy(
+                out=cropped[:].rearrange("p (d h w) -> p d h w", h=UP * HEIGHT, w=UP * WIDTH),
+                in_=z_raws[i][:].rearrange("p (d h w) -> p d h w", h=Z_HEIGHT, w=Z_WIDTH)[
+                    :, :, MARGIN : MARGIN + UP * HEIGHT, MARGIN : MARGIN + UP * WIDTH
+                ],
+            )
+            nc.sync.dma_start(out=out_rows[OUT_CHANNELS + i * P : OUT_CHANNELS + (i + 1) * P, :], in_=cropped[:])
+
+        b_rows = const.tile([P, P], BF16)
+        nc.vector.memset(b_rows[:], 0.0)
+        nc.scalar.dma_start(out=b_rows[0:O_TILES, :], in_=b.rearrange("(m o) -> m o", m=O_TILES))
+        b_rows_f32 = const.tile([P, P], F32)
+        nc.vector.tensor_copy(out=b_rows_f32[:], in_=b_rows[:])
+
+        ready = quantise_chunk(transpose_chunk(0))
+
+        b_turned = turned_pool.tile([P, BANK_WORDS], F32, tag="turned")
+        nc.tensor.transpose(out=b_turned[:, 0:P], in_=b_rows_f32[:], identity=identity[:])
+        bias = const.tile([P, O_TILES], F32)
+        nc.scalar.activation(out=bias[:], in_=b_turned[:, 0:O_TILES], func=IDENTITY)
+
+        acc = []
+        for q in range(ALL_CHUNKS):
+            m, n = divmod(q, CHUNKS)
+            quantised = ready
+            if q + 1 < ALL_CHUNKS:
+                banks = transpose_chunk(q + 1)
+            if m == 0:
+                for piece in range(n * RUN_PIECES, (n + 1) * RUN_PIECES):
+                    prepare_x(piece)
+            if q + 1 < ALL_CHUNKS:
+                ready = quantise_chunk(banks)
+            if n == 0:
+                acc = []
+                for j in range(GROUPS):
+                    group = acc_pool.tile([P, N_MOVING], F32)
+                    acc.append(group)
+            multiply(n, quantised, acc)
+            if m == Z_O_TILE:
+                for i in range(n * Z_TILES // CHUNKS, (n + 1) * Z_TILES // CHUNKS):
+                    crop_z(i)
+            if n == CHUNKS - 1:
+                finish(m, acc)

@@ -10,6 +10,7 @@ U8 = mybir.dt.uint8
 FP8X4 = mybir.dt.float8_e4m3fn_x4
 IDENTITY = mybir.ActivationFunctionType.Identity
 
+
 P = 128
 PACK = 4
 K_PASS = P * PACK
@@ -39,13 +40,10 @@ GROUPS = UP * UP
 
 PIECE_PASSES = 4
 PIECE_K = PIECE_PASSES * K_PASS
+PIECE_WORDS = PIECE_K // PAIR
 PIECES = PASSES // PIECE_PASSES
-PIECE_BANKS = PIECE_K // PAIR // BANK_WORDS
+PIECE_BANKS = PIECE_WORDS // BANK_WORDS
 BANK_PASSES = PIECE_PASSES // PIECE_BANKS
-RUN_PIECES = (PSUM_BANKS - GROUPS) // PIECE_BANKS
-CHUNKS = PIECES // RUN_PIECES
-ALL_CHUNKS = O_TILES * CHUNKS
-Z_O_TILE = 2
 
 FLOPS = 2 * OUT_CHANNELS * CHANNELS * UP_POSITIONS
 BYTES = (
@@ -66,33 +64,30 @@ def tile_upconvcropcat_k_kernel(tc, x, z, W, b, out):
         w_raw_pool = stack.enter_context(tc.tile_pool(name="w_raw", bufs=O_TILES * PIECES))
         z_raw_pool = stack.enter_context(tc.tile_pool(name="z_raw", bufs=Z_TILES))
         x_mx_pool = stack.enter_context(tc.tile_pool(name="x_mx", bufs=PIECES))
-        stage = stack.enter_context(tc.tile_pool(name="stage", bufs=3 * RUN_PIECES))
+        stage = stack.enter_context(tc.tile_pool(name="stage", bufs=6))
         results = stack.enter_context(tc.tile_pool(name="results", bufs=4))
         acc_pool = stack.enter_context(tc.psum_pool(name="acc", bufs=GROUPS))
         turned_pool = stack.enter_context(tc.psum_pool(name="turned", bufs=PSUM_BANKS - GROUPS))
         stack.enter_context(tc.manual_schedule())
 
         x_raws = []
-        w_raws = []
+        w_raws = {}
         z_raws = []
 
-        def load_w_chunk(q):
-            m, n = divmod(q, CHUNKS)
-            for piece in range(n * RUN_PIECES, (n + 1) * RUN_PIECES):
-                w_raw = w_raw_pool.tile([P, PIECE_K], BF16)
-                nc.sync.dma_start(out=w_raw[:], in_=W[m * P : (m + 1) * P, piece * PIECE_K : (piece + 1) * PIECE_K])
-                w_raws.append(w_raw)
+        def load_w(m, piece):
+            w_raw = w_raw_pool.tile([P, PIECE_K], BF16)
+            nc.sync.dma_start(out=w_raw[:], in_=W[m * P : (m + 1) * P, piece * PIECE_K : (piece + 1) * PIECE_K])
+            w_raws[m, piece] = w_raw
 
-        def load_x_chunk(n):
-            for piece in range(n * RUN_PIECES, (n + 1) * RUN_PIECES):
-                x_raw = x_raw_pool.tile([P, PIECE_K], BF16)
-                nc.sync.dma_start(
-                    out=x_raw[:].rearrange("p (g f) -> p g f", f=PACK * POSITIONS),
-                    in_=x_rows[piece * PIECE_K : (piece + 1) * PIECE_K, :].rearrange(
-                        "(g q t) w -> q g (t w)", q=P, t=PACK
-                    ),
-                )
-                x_raws.append(x_raw)
+        def load_x(piece):
+            x_raw = x_raw_pool.tile([P, PIECE_K], BF16)
+            nc.sync.dma_start(
+                out=x_raw[:].rearrange("p (g f) -> p g f", f=PACK * POSITIONS),
+                in_=x_rows[piece * PIECE_K : (piece + 1) * PIECE_K, :].rearrange(
+                    "(g q t) w -> q g (t w)", q=P, t=PACK
+                ),
+            )
+            x_raws.append(x_raw)
 
         def load_z(i):
             z_raw = z_raw_pool.tile([P, UP * DEPTH * Z_HEIGHT * Z_WIDTH], BF16)
@@ -102,61 +97,74 @@ def tile_upconvcropcat_k_kernel(tc, x, z, W, b, out):
             )
             z_raws.append(z_raw)
 
-        load_w_chunk(0)
-        load_w_chunk(1)
-        for q in range(ALL_CHUNKS - 2):
-            if q < CHUNKS:
-                load_x_chunk(q)
-            if q + 2 == (O_TILES - 1) * CHUNKS:
+        for piece in range(PIECES):
+            load_w(0, piece)
+            load_x(piece)
+        for m in range(1, O_TILES):
+            for piece in range(PIECES):
+                load_w(m, piece)
+            if m == 1:
                 for i in range(Z_TILES):
                     load_z(i)
-            load_w_chunk(q + 2)
 
         identity = const.tile([P, P], F32)
         make_identity(nc, identity[:])
 
-        def transpose_chunk(q):
+        ordered_words = {}
+
+        def order(m, piece):
+            w_ordered = stage.tile([P, PIECE_K], BF16, align_bytes=64)
+            nc.scalar.copy(
+                out=w_ordered[:].bitcast(F32).rearrange("p (g u q) -> p g u q", g=PIECE_PASSES, u=PAIR),
+                in_=w_raws[m, piece][:].bitcast(F32).rearrange("p (g q u) -> p g u q", g=PIECE_PASSES, u=PAIR),
+            )
+            ordered_words[m, piece] = w_ordered
+
+        turned_banks = {}
+
+        def transpose(m, piece):
             banks = []
-            for w_raw in w_raws[q * RUN_PIECES : (q + 1) * RUN_PIECES]:
-                raw_words = w_raw[:].bitcast(F32)
-                for h in range(PIECE_BANKS):
-                    turned = turned_pool.tile([P, BANK_WORDS], F32, tag="turned")
-                    for s in range(BANK_WORDS // P):
+            for h in range(PIECE_BANKS):
+                turned = turned_pool.tile([P, BANK_WORDS], F32, tag="turned")
+                for s in range(BANK_WORDS // P):
+                    if m == 0:
                         g, u = divmod(s, PAIR)
                         first = h * BANK_WORDS + g * PAIR * P
-                        nc.tensor.transpose(
-                            out=turned[:, s * P : (s + 1) * P],
-                            in_=raw_words[:, first + u : first + PAIR * P : PAIR],
-                            identity=identity[:],
-                        )
-                    banks.append(turned)
-            return banks
+                        words = w_raws[m, piece][:].bitcast(F32)[:, first + u : first + PAIR * P : PAIR]
+                    else:
+                        first = h * BANK_WORDS + s * P
+                        words = ordered_words[m, piece][:].bitcast(F32)[:, first : first + P]
+                    nc.tensor.transpose(out=turned[:, s * P : (s + 1) * P], in_=words, identity=identity[:])
+                banks.append(turned)
+            turned_banks[m, piece] = banks
 
-        def quantise_chunk(banks):
-            grouped = []
-            for i in range(RUN_PIECES):
-                w_grouped = stage.tile([P, PIECE_K], BF16, align_bytes=64)
-                grouped_words = w_grouped[:].bitcast(F32)
-                for h in range(PIECE_BANKS):
-                    copy = nc.scalar.copy if h == 0 else nc.vector.tensor_copy
-                    copy(
-                        out=grouped_words[:, h * BANK_WORDS : (h + 1) * BANK_WORDS].rearrange(
-                            "p (g o u) -> p g o u", g=BANK_PASSES, u=PAIR
-                        ),
-                        in_=banks[i * PIECE_BANKS + h][:].rearrange("p (g u o) -> p g o u", g=BANK_PASSES, u=PAIR),
-                    )
-                grouped.append(w_grouped)
-            quantised = []
-            for w_grouped in grouped:
-                w_words = stage.tile([P, PIECE_PASSES * P], U32, align_bytes=64)
-                w_scales = stage.tile([P, PIECE_PASSES * P], U8, align_bytes=64)
-                nc.vector.quantize_mx(out=w_words[:].bitcast(FP8X4), scales=w_scales[:], in_=w_grouped[:])
-                quantised.append((w_words, w_scales))
-            return quantised
+        w_groups = {}
 
+        def copy_out(m, piece):
+            w_grouped = stage.tile([P, PIECE_K], BF16, align_bytes=64)
+            grouped_words = w_grouped[:].bitcast(F32)
+            for h in range(PIECE_BANKS):
+                copy = nc.scalar.copy if h == 0 else nc.vector.tensor_copy
+                copy(
+                    out=grouped_words[:, h * BANK_WORDS : (h + 1) * BANK_WORDS].rearrange(
+                        "p (g o u) -> p g o u", g=BANK_PASSES, u=PAIR
+                    ),
+                    in_=turned_banks[m, piece][h][:].rearrange("p (g u o) -> p g o u", g=BANK_PASSES, u=PAIR),
+                )
+            w_groups[m, piece] = w_grouped
+
+        w_quantised = {}
+
+        def quantise(m, piece):
+            w_words = stage.tile([P, PIECE_PASSES * P], U32, align_bytes=64)
+            w_scales = stage.tile([P, PIECE_PASSES * P], U8, align_bytes=64)
+            nc.vector.quantize_mx(out=w_words[:].bitcast(FP8X4), scales=w_scales[:], in_=w_groups[m, piece][:])
+            w_quantised[m, piece] = (w_words, w_scales)
+
+        x_groups = []
         x_quantised = []
 
-        def prepare_x(piece):
+        def group_x(piece):
             x_grouped = stage.tile([P, PIECE_K], BF16, align_bytes=64)
             for g in range(PIECE_PASSES):
                 cols = slice(g * K_PASS, (g + 1) * K_PASS)
@@ -165,6 +173,9 @@ def tile_upconvcropcat_k_kernel(tc, x, z, W, b, out):
                     out=x_grouped[:, cols].rearrange("p (c i t) -> p c t i", i=4, t=PACK),
                     in_=x_raws[piece][:, cols].rearrange("p (t c i) -> p c t i", t=PACK, i=4),
                 )
+            x_groups.append(x_grouped)
+
+        def quantise_x(piece):
             x_words = x_mx_pool.tile([P, PIECE_PASSES * N_MOVING], U32, align_bytes=64)
             x_scales = x_mx_pool.tile([P, PIECE_PASSES * N_MOVING], U8, align_bytes=64)
             for g in range(PIECE_PASSES):
@@ -173,36 +184,42 @@ def tile_upconvcropcat_k_kernel(tc, x, z, W, b, out):
                     nc.vector.quantize_mx(
                         out=x_words[:, cols].bitcast(FP8X4),
                         scales=x_scales[:, cols],
-                        in_=x_grouped[:, g * K_PASS : (g + 1) * K_PASS],
+                        in_=x_groups[piece][:, g * K_PASS : (g + 1) * K_PASS],
                     )
             x_quantised.append((x_words, x_scales))
 
-        def multiply(n, quantised, acc):
-            for i in range(RUN_PIECES):
-                w_words, w_scales = quantised[i]
-                x_words, x_scales = x_quantised[n * RUN_PIECES + i]
-                for g in range(PIECE_PASSES):
-                    c = (n * RUN_PIECES + i) * PIECE_PASSES + g
-                    o_cols = slice(g * P, (g + 1) * P)
-                    x_cols = slice(g * N_MOVING, (g + 1) * N_MOVING)
-                    for group in acc:
-                        nc.tensor.matmul_mx(
-                            out=group[:],
-                            lhsT=w_words[:, o_cols].bitcast(FP8X4),
-                            lhsT_scale=w_scales[:, o_cols],
-                            rhs=x_words[:, x_cols].bitcast(FP8X4),
-                            rhs_scale=x_scales[:, x_cols],
-                            start=(c == 0),
-                            stop=(c == PASSES - 1),
-                        )
+        accs = {}
 
-        def finish(m, acc):
+        def multiply(m, piece):
+            if piece == 0:
+                accs[m] = []
+                for j in range(GROUPS):
+                    group = acc_pool.tile([P, N_MOVING], F32)
+                    accs[m].append(group)
+            w_words, w_scales = w_quantised[m, piece]
+            x_words, x_scales = x_quantised[piece]
+            for g in range(PIECE_PASSES):
+                c = piece * PIECE_PASSES + g
+                o_cols = slice(g * P, (g + 1) * P)
+                x_cols = slice(g * N_MOVING, (g + 1) * N_MOVING)
+                for group in accs[m]:
+                    nc.tensor.matmul_mx(
+                        out=group[:],
+                        lhsT=w_words[:, o_cols].bitcast(FP8X4),
+                        lhsT_scale=w_scales[:, o_cols],
+                        rhs=x_words[:, x_cols].bitcast(FP8X4),
+                        rhs_scale=x_scales[:, x_cols],
+                        start=(c == 0),
+                        stop=(c == PASSES - 1),
+                    )
+
+        def finish(m):
             planes = out_rows[m * P : (m + 1) * P, :].rearrange("o (i a f) -> o a i f", i=DEPTH, a=UP)
             for a in range(UP):
                 y = results.tile([P, DEPTH * UP_PLANE], F32)
                 y_view = y[:].rearrange("p (i h b k r) -> p b i h k r", i=DEPTH, h=HEIGHT, b=UP, k=WIDTH, r=UP)
                 for bb in range(UP):
-                    sums = acc[a * UP + bb][:].rearrange("p (r i h k) -> p i h k r", r=UP, i=DEPTH, h=HEIGHT)
+                    sums = accs[m][a * UP + bb][:].rearrange("p (r i h k) -> p i h k r", r=UP, i=DEPTH, h=HEIGHT)
                     if bb == 0:
                         nc.scalar.activation(out=y_view[:, bb], in_=sums, func=IDENTITY, bias=bias[:, m : m + 1])
                     else:
@@ -223,34 +240,53 @@ def tile_upconvcropcat_k_kernel(tc, x, z, W, b, out):
         nc.vector.memset(b_rows[:], 0.0)
         nc.scalar.dma_start(out=b_rows[0:O_TILES, :], in_=b.rearrange("(m o) -> m o", m=O_TILES))
         b_rows_f32 = const.tile([P, P], F32)
-        nc.vector.tensor_copy(out=b_rows_f32[:], in_=b_rows[:])
-
-        ready = quantise_chunk(transpose_chunk(0))
-
-        b_turned = turned_pool.tile([P, BANK_WORDS], F32, tag="turned")
-        nc.tensor.transpose(out=b_turned[:, 0:P], in_=b_rows_f32[:], identity=identity[:])
         bias = const.tile([P, O_TILES], F32)
-        nc.scalar.activation(out=bias[:], in_=b_turned[:, 0:O_TILES], func=IDENTITY)
 
-        acc = []
-        for q in range(ALL_CHUNKS):
-            m, n = divmod(q, CHUNKS)
-            quantised = ready
-            if q + 1 < ALL_CHUNKS:
-                banks = transpose_chunk(q + 1)
-            if m == 0:
-                for piece in range(n * RUN_PIECES, (n + 1) * RUN_PIECES):
-                    prepare_x(piece)
-            if q + 1 < ALL_CHUNKS:
-                ready = quantise_chunk(banks)
-            if n == 0:
-                acc = []
-                for j in range(GROUPS):
-                    group = acc_pool.tile([P, N_MOVING], F32)
-                    acc.append(group)
-            multiply(n, quantised, acc)
-            if m == Z_O_TILE:
-                for i in range(n * Z_TILES // CHUNKS, (n + 1) * Z_TILES // CHUNKS):
-                    crop_z(i)
-            if n == CHUNKS - 1:
-                finish(m, acc)
+        def turn_bias():
+            nc.vector.tensor_copy(out=b_rows_f32[:], in_=b_rows[:])
+            b_turned = turned_pool.tile([P, BANK_WORDS], F32, tag="turned")
+            nc.tensor.transpose(out=b_turned[:, 0:P], in_=b_rows_f32[:], identity=identity[:])
+            nc.scalar.activation(out=bias[:], in_=b_turned[:, 0:O_TILES], func=IDENTITY)
+
+        def prepare(m, piece):
+            copy_out(m, piece)
+            group_x(piece)
+            quantise(m, piece)
+            quantise_x(piece)
+
+        transpose(0, 0)
+        prepare(0, 0)
+        transpose(0, 1)
+        for piece in range(1, PIECES):
+            prepare(0, piece)
+            multiply(0, piece - 1)
+            if piece + 1 < PIECES:
+                transpose(0, piece + 1)
+        turn_bias()
+        runs = []
+        for m in range(1, O_TILES):
+            for piece in range(0, PIECES, 2):
+                runs.append(((m, piece), (m, piece + 1)))
+        for step in runs[0]:
+            order(*step)
+        waiting = [(0, PIECES - 1)]
+        for j, run in enumerate(runs):
+            for step in run:
+                transpose(*step)
+            for step in run:
+                copy_out(*step)
+            if j + 1 < len(runs):
+                for step in runs[j + 1]:
+                    order(*step)
+            for step in run:
+                quantise(*step)
+            for step in waiting:
+                multiply(*step)
+                if step[1] == PIECES - 1:
+                    finish(step[0])
+            if j in (1, 2, 3, 4):
+                crop_z(j - 1)
+            waiting = run
+        for step in waiting:
+            multiply(*step)
+        finish(O_TILES - 1)

@@ -64,7 +64,7 @@ def tile_upconvcropcat_k_kernel(tc, x, z, W, b, out):
         w_raw_pool = stack.enter_context(tc.tile_pool(name="w_raw", bufs=O_TILES * PIECES))
         z_raw_pool = stack.enter_context(tc.tile_pool(name="z_raw", bufs=Z_TILES))
         x_mx_pool = stack.enter_context(tc.tile_pool(name="x_mx", bufs=PIECES))
-        stage = stack.enter_context(tc.tile_pool(name="stage", bufs=6))
+        stage = stack.enter_context(tc.tile_pool(name="stage", bufs=4))
         results = stack.enter_context(tc.tile_pool(name="results", bufs=4))
         acc_pool = stack.enter_context(tc.psum_pool(name="acc", bufs=GROUPS))
         turned_pool = stack.enter_context(tc.psum_pool(name="turned", bufs=PSUM_BANKS - GROUPS))
@@ -74,20 +74,26 @@ def tile_upconvcropcat_k_kernel(tc, x, z, W, b, out):
         w_raws = {}
         z_raws = []
 
-        def load_w(m, piece):
-            w_raw = w_raw_pool.tile([P, PIECE_K], BF16)
-            nc.sync.dma_start(out=w_raw[:], in_=W[m * P : (m + 1) * P, piece * PIECE_K : (piece + 1) * PIECE_K])
-            w_raws[m, piece] = w_raw
-
-        def load_x(piece):
-            x_raw = x_raw_pool.tile([P, PIECE_K], BF16)
+        def load_w(m, piece, passes):
+            if passes[0] == 0:
+                w_raw = w_raw_pool.tile([P, PIECE_K], BF16)
+                w_raws[m, piece] = w_raw
+            cols = slice(passes[0] * K_PASS, (passes[-1] + 1) * K_PASS)
             nc.sync.dma_start(
-                out=x_raw[:].rearrange("p (g f) -> p g f", f=PACK * POSITIONS),
-                in_=x_rows[piece * PIECE_K : (piece + 1) * PIECE_K, :].rearrange(
-                    "(g q t) w -> q g (t w)", q=P, t=PACK
-                ),
+                out=w_raws[m, piece][:, cols],
+                in_=W[m * P : (m + 1) * P, piece * PIECE_K + cols.start : piece * PIECE_K + cols.stop],
             )
-            x_raws.append(x_raw)
+
+        def load_x(piece, passes):
+            if passes[0] == 0:
+                x_raw = x_raw_pool.tile([P, PIECE_K], BF16)
+                x_raws.append(x_raw)
+            cols = slice(passes[0] * K_PASS, (passes[-1] + 1) * K_PASS)
+            first = piece * PIECE_K
+            nc.sync.dma_start(
+                out=x_raws[piece][:, cols].rearrange("p (g f) -> p g f", f=PACK * POSITIONS),
+                in_=x_rows[first + cols.start : first + cols.stop, :].rearrange("(g q t) w -> q g (t w)", q=P, t=PACK),
+            )
 
         def load_z(i):
             z_raw = z_raw_pool.tile([P, UP * DEPTH * Z_HEIGHT * Z_WIDTH], BF16)
@@ -97,24 +103,31 @@ def tile_upconvcropcat_k_kernel(tc, x, z, W, b, out):
             )
             z_raws.append(z_raw)
 
-        for piece in range(PIECES):
-            load_w(0, piece)
-            load_x(piece)
+        first, last, every = (0, 1), (2, 3), (0, 1, 2, 3)
+        load_w(0, 0, first)
+        load_x(0, first)
+        load_w(0, 0, last)
+        load_x(0, last)
+        for piece in range(1, PIECES):
+            load_w(0, piece, every)
+            load_x(piece, every)
         for m in range(1, O_TILES):
             for piece in range(PIECES):
-                load_w(m, piece)
+                load_w(m, piece, every)
             if m == 1:
                 for i in range(Z_TILES):
                     load_z(i)
 
+        vector_copy = nc.vector.tensor_copy
+        scalar_copy = nc.scalar.copy
         identity = const.tile([P, P], F32)
         make_identity(nc, identity[:])
 
         ordered_words = {}
 
-        def order(m, piece):
+        def order(m, piece, copy):
             w_ordered = stage.tile([P, PIECE_K], BF16, align_bytes=64)
-            nc.scalar.copy(
+            copy(
                 out=w_ordered[:].bitcast(F32).rearrange("p (g u q) -> p g u q", g=PIECE_PASSES, u=PAIR),
                 in_=w_raws[m, piece][:].bitcast(F32).rearrange("p (g q u) -> p g u q", g=PIECE_PASSES, u=PAIR),
             )
@@ -127,25 +140,24 @@ def tile_upconvcropcat_k_kernel(tc, x, z, W, b, out):
             for h in range(PIECE_BANKS):
                 turned = turned_pool.tile([P, BANK_WORDS], F32, tag="turned")
                 for s in range(BANK_WORDS // P):
-                    if m == 0:
-                        g, u = divmod(s, PAIR)
-                        first = h * BANK_WORDS + g * PAIR * P
-                        words = w_raws[m, piece][:].bitcast(F32)[:, first + u : first + PAIR * P : PAIR]
+                    if (m, piece) in ordered_words:
+                        first_word = h * BANK_WORDS + s * P
+                        words = ordered_words[m, piece][:].bitcast(F32)[:, first_word : first_word + P]
                     else:
-                        first = h * BANK_WORDS + s * P
-                        words = ordered_words[m, piece][:].bitcast(F32)[:, first : first + P]
+                        g, u = divmod(s, PAIR)
+                        first_word = h * BANK_WORDS + g * PAIR * P
+                        words = w_raws[m, piece][:].bitcast(F32)[:, first_word + u : first_word + PAIR * P : PAIR]
                     nc.tensor.transpose(out=turned[:, s * P : (s + 1) * P], in_=words, identity=identity[:])
                 banks.append(turned)
             turned_banks[m, piece] = banks
 
         w_groups = {}
 
-        def copy_out(m, piece):
+        def copy_out(m, piece, copies):
             w_grouped = stage.tile([P, PIECE_K], BF16, align_bytes=64)
             grouped_words = w_grouped[:].bitcast(F32)
             for h in range(PIECE_BANKS):
-                copy = nc.scalar.copy if h == 0 else nc.vector.tensor_copy
-                copy(
+                copies[h](
                     out=grouped_words[:, h * BANK_WORDS : (h + 1) * BANK_WORDS].rearrange(
                         "p (g o u) -> p g o u", g=BANK_PASSES, u=PAIR
                     ),
@@ -155,63 +167,72 @@ def tile_upconvcropcat_k_kernel(tc, x, z, W, b, out):
 
         w_quantised = {}
 
-        def quantise(m, piece):
-            w_words = stage.tile([P, PIECE_PASSES * P], U32, align_bytes=64)
-            w_scales = stage.tile([P, PIECE_PASSES * P], U8, align_bytes=64)
-            nc.vector.quantize_mx(out=w_words[:].bitcast(FP8X4), scales=w_scales[:], in_=w_groups[m, piece][:])
-            w_quantised[m, piece] = (w_words, w_scales)
+        def quantise(m, piece, passes):
+            if passes[0] == 0:
+                w_words = stage.tile([P, PIECE_PASSES * P], U32, bufs=8, align_bytes=64)
+                w_scales = stage.tile([P, PIECE_PASSES * P], U8, bufs=8, align_bytes=64)
+                w_quantised[m, piece] = (w_words, w_scales)
+            w_words, w_scales = w_quantised[m, piece]
+            cols = slice(passes[0] * P, (passes[-1] + 1) * P)
+            nc.vector.quantize_mx(
+                out=w_words[:, cols].bitcast(FP8X4),
+                scales=w_scales[:, cols],
+                in_=w_groups[m, piece][:, passes[0] * K_PASS : (passes[-1] + 1) * K_PASS],
+            )
 
         x_groups = []
         x_quantised = []
 
-        def group_x(piece):
-            x_grouped = stage.tile([P, PIECE_K], BF16, align_bytes=64)
-            for g in range(PIECE_PASSES):
-                cols = slice(g * K_PASS, (g + 1) * K_PASS)
-                copy = nc.vector.tensor_copy if g % 2 == 0 else nc.scalar.copy
-                copy(
-                    out=x_grouped[:, cols].rearrange("p (c i t) -> p c t i", i=4, t=PACK),
-                    in_=x_raws[piece][:, cols].rearrange("p (t c i) -> p c t i", t=PACK, i=4),
-                )
-            x_groups.append(x_grouped)
+        def group_x(piece, g, copy):
+            if g == 0:
+                x_grouped = stage.tile([P, PIECE_K], BF16, bufs=3, align_bytes=64)
+                x_groups.append(x_grouped)
+            cols = slice(g * K_PASS, (g + 1) * K_PASS)
+            copy(
+                out=x_groups[piece][:, cols].rearrange("p (c i t) -> p c t i", i=4, t=PACK),
+                in_=x_raws[piece][:, cols].rearrange("p (t c i) -> p c t i", t=PACK, i=4),
+            )
 
-        def quantise_x(piece):
-            x_words = x_mx_pool.tile([P, PIECE_PASSES * N_MOVING], U32, align_bytes=64)
-            x_scales = x_mx_pool.tile([P, PIECE_PASSES * N_MOVING], U8, align_bytes=64)
-            for g in range(PIECE_PASSES):
-                for r in range(UP):
-                    cols = slice(g * N_MOVING + r * POSITIONS, g * N_MOVING + (r + 1) * POSITIONS)
-                    nc.vector.quantize_mx(
-                        out=x_words[:, cols].bitcast(FP8X4),
-                        scales=x_scales[:, cols],
-                        in_=x_groups[piece][:, g * K_PASS : (g + 1) * K_PASS],
-                    )
-            x_quantised.append((x_words, x_scales))
+        def quantise_x(piece, g):
+            if g == 0:
+                x_words = x_mx_pool.tile([P, PIECE_PASSES * N_MOVING], U32, align_bytes=64)
+                x_scales = x_mx_pool.tile([P, PIECE_PASSES * N_MOVING], U8, align_bytes=64)
+                x_quantised.append((x_words, x_scales))
+            x_words, x_scales = x_quantised[piece]
+            for r in range(UP):
+                cols = slice(g * N_MOVING + r * POSITIONS, g * N_MOVING + (r + 1) * POSITIONS)
+                nc.vector.quantize_mx(
+                    out=x_words[:, cols].bitcast(FP8X4),
+                    scales=x_scales[:, cols],
+                    in_=x_groups[piece][:, g * K_PASS : (g + 1) * K_PASS],
+                )
 
         accs = {}
 
-        def multiply(m, piece):
-            if piece == 0:
+        def multiply(m, piece, passes):
+            if piece == 0 and passes[0] == 0:
                 accs[m] = []
                 for j in range(GROUPS):
                     group = acc_pool.tile([P, N_MOVING], F32)
                     accs[m].append(group)
             w_words, w_scales = w_quantised[m, piece]
             x_words, x_scales = x_quantised[piece]
-            for g in range(PIECE_PASSES):
+            steps = [(g, j) for g in passes for j in range(GROUPS)]
+            if (m, piece) == (O_TILES - 1, PIECES - 1):
+                steps = [(g, j) for j in range(GROUPS) for g in passes]
+            for g, j in steps:
                 c = piece * PIECE_PASSES + g
                 o_cols = slice(g * P, (g + 1) * P)
                 x_cols = slice(g * N_MOVING, (g + 1) * N_MOVING)
-                for group in accs[m]:
-                    nc.tensor.matmul_mx(
-                        out=group[:],
-                        lhsT=w_words[:, o_cols].bitcast(FP8X4),
-                        lhsT_scale=w_scales[:, o_cols],
-                        rhs=x_words[:, x_cols].bitcast(FP8X4),
-                        rhs_scale=x_scales[:, x_cols],
-                        start=(c == 0),
-                        stop=(c == PASSES - 1),
-                    )
+                nc.tensor.matmul_mx(
+                    out=accs[m][j][:],
+                    lhsT=w_words[:, o_cols].bitcast(FP8X4),
+                    lhsT_scale=w_scales[:, o_cols],
+                    rhs=x_words[:, x_cols].bitcast(FP8X4),
+                    rhs_scale=x_scales[:, x_cols],
+                    start=(c == 0),
+                    stop=(c == PASSES - 1),
+                )
 
         def finish(m):
             planes = out_rows[m * P : (m + 1) * P, :].rearrange("o (i a f) -> o a i f", i=DEPTH, a=UP)
@@ -226,9 +247,9 @@ def tile_upconvcropcat_k_kernel(tc, x, z, W, b, out):
                         nc.vector.tensor_scalar_add(out=y_view[:, bb], in0=sums, scalar1=bias[:, m : m + 1])
                 nc.sync.dma_start(out=planes[:, a], in_=y[:].rearrange("p (i f) -> p i f", i=DEPTH))
 
-        def crop_z(i):
+        def crop_z(i, copy):
             cropped = results.tile([P, UP_POSITIONS], F32)
-            nc.vector.tensor_copy(
+            copy(
                 out=cropped[:].rearrange("p (d h w) -> p d h w", h=UP * HEIGHT, w=UP * WIDTH),
                 in_=z_raws[i][:].rearrange("p (d h w) -> p d h w", h=Z_HEIGHT, w=Z_WIDTH)[
                     :, :, MARGIN : MARGIN + UP * HEIGHT, MARGIN : MARGIN + UP * WIDTH
@@ -243,50 +264,65 @@ def tile_upconvcropcat_k_kernel(tc, x, z, W, b, out):
         bias = const.tile([P, O_TILES], F32)
 
         def turn_bias():
-            nc.vector.tensor_copy(out=b_rows_f32[:], in_=b_rows[:])
             b_turned = turned_pool.tile([P, BANK_WORDS], F32, tag="turned")
             nc.tensor.transpose(out=b_turned[:, 0:P], in_=b_rows_f32[:], identity=identity[:])
-            nc.scalar.activation(out=bias[:], in_=b_turned[:, 0:O_TILES], func=IDENTITY)
+            return b_turned
 
-        def prepare(m, piece):
-            copy_out(m, piece)
-            group_x(piece)
-            quantise(m, piece)
-            quantise_x(piece)
-
+        both = (scalar_copy, vector_copy)
+        warm = const.tile([P, 1], F32)
+        nc.scalar.activation(out=warm[:], in_=identity[:, 0:1], func=IDENTITY)
         transpose(0, 0)
-        prepare(0, 0)
+        group_x(0, 0, scalar_copy)
+        copy_out(0, 0, (vector_copy, scalar_copy))
+        quantise(0, 0, first)
+        quantise_x(0, 0)
+        group_x(0, 1, scalar_copy)
+        quantise(0, 0, last)
+        quantise_x(0, 1)
+        nc.vector.tensor_copy(out=b_rows_f32[:], in_=b_rows[:])
+        multiply(0, 0, first)
         transpose(0, 1)
+        b_turned = turn_bias()
+        group_x(0, 2, scalar_copy)
+        group_x(0, 3, vector_copy)
+        quantise_x(0, 2)
+        quantise_x(0, 3)
+        multiply(0, 0, last)
         for piece in range(1, PIECES):
-            prepare(0, piece)
-            multiply(0, piece - 1)
+            copy_out(0, piece, both)
+            group_x(piece, 0, vector_copy)
+            quantise(0, piece, every)
+            for g in every:
+                if g > 0:
+                    group_x(piece, g, scalar_copy)
+                quantise_x(piece, g)
+            if piece == 1:
+                nc.scalar.activation(out=bias[:], in_=b_turned[:, 0:O_TILES], func=IDENTITY)
             if piece + 1 < PIECES:
                 transpose(0, piece + 1)
-        turn_bias()
+                multiply(0, piece, every)
         runs = []
         for m in range(1, O_TILES):
             for piece in range(0, PIECES, 2):
                 runs.append(((m, piece), (m, piece + 1)))
-        for step in runs[0]:
-            order(*step)
         waiting = [(0, PIECES - 1)]
         for j, run in enumerate(runs):
             for step in run:
                 transpose(*step)
             for step in run:
-                copy_out(*step)
+                copy_out(*step, both)
             if j + 1 < len(runs):
                 for step in runs[j + 1]:
-                    order(*step)
+                    order(*step, scalar_copy)
             for step in run:
-                quantise(*step)
+                quantise(*step, every)
             for step in waiting:
-                multiply(*step)
+                multiply(*step, every)
                 if step[1] == PIECES - 1:
                     finish(step[0])
             if j in (1, 2, 3, 4):
-                crop_z(j - 1)
+                crop_z(j - 1, vector_copy)
             waiting = run
         for step in waiting:
-            multiply(*step)
+            multiply(*step, every)
         finish(O_TILES - 1)

@@ -108,9 +108,12 @@ def tile_upconvcropcat_k_kernel(tc, x, z, W, b, out):
         load_x(0, first)
         load_w(0, 0, last)
         load_x(0, last)
-        for piece in range(1, PIECES):
-            load_w(0, piece, every)
-            load_x(piece, every)
+        load_w(0, 1, every)
+        load_w(0, 2, every)
+        load_x(1, every)
+        load_x(2, every)
+        load_w(0, 3, every)
+        load_x(3, every)
         for m in range(1, O_TILES):
             for piece in range(PIECES):
                 load_w(m, piece, every)
@@ -135,9 +138,9 @@ def tile_upconvcropcat_k_kernel(tc, x, z, W, b, out):
 
         turned_banks = {}
 
-        def transpose(m, piece):
-            banks = []
-            for h in range(PIECE_BANKS):
+        def transpose(m, piece, halves=(0, 1)):
+            banks = turned_banks.setdefault((m, piece), [])
+            for h in halves:
                 turned = turned_pool.tile([P, BANK_WORDS], F32, tag="turned")
                 for s in range(BANK_WORDS // P):
                     if (m, piece) in ordered_words:
@@ -149,7 +152,14 @@ def tile_upconvcropcat_k_kernel(tc, x, z, W, b, out):
                         words = w_raws[m, piece][:].bitcast(F32)[:, first_word + u : first_word + PAIR * P : PAIR]
                     nc.tensor.transpose(out=turned[:, s * P : (s + 1) * P], in_=words, identity=identity[:])
                 banks.append(turned)
-            turned_banks[m, piece] = banks
+
+        zeros = const.tile([P, BANK_WORDS], BF16)
+        nc.vector.memset(zeros[:], 0.0)
+        idle_bank = turned_pool.tile([P, BANK_WORDS], F32, tag="turned")
+
+        def keep_busy(count):
+            for k in range(count):
+                nc.tensor.matmul(out=idle_bank[:], lhsT=zeros[:, 0:P], rhs=zeros[:], start=True, stop=True)
 
         w_groups = {}
 
@@ -239,13 +249,24 @@ def tile_upconvcropcat_k_kernel(tc, x, z, W, b, out):
             for a in range(UP):
                 y = results.tile([P, DEPTH * UP_PLANE], F32)
                 y_view = y[:].rearrange("p (i h b k r) -> p b i h k r", i=DEPTH, h=HEIGHT, b=UP, k=WIDTH, r=UP)
+                views = []
                 for bb in range(UP):
                     sums = accs[m][a * UP + bb][:].rearrange("p (r i h k) -> p i h k r", r=UP, i=DEPTH, h=HEIGHT)
-                    if bb == 0:
-                        nc.scalar.activation(out=y_view[:, bb], in_=sums, func=IDENTITY, bias=bias[:, m : m + 1])
+                    if (m, a) == (O_TILES - 1, UP - 1):
+                        views.append((y_view[:, bb, 0], sums[:, 0], True))
+                        views.append((y_view[:, bb, 1], sums[:, 1], False))
                     else:
-                        nc.vector.tensor_scalar_add(out=y_view[:, bb], in0=sums, scalar1=bias[:, m : m + 1])
-                nc.sync.dma_start(out=planes[:, a], in_=y[:].rearrange("p (i f) -> p i f", i=DEPTH))
+                        views.append((y_view[:, bb], sums, bb == 0))
+                for y_part, sums, on_scalar in views:
+                    if on_scalar:
+                        nc.scalar.activation(out=y_part, in_=sums, func=IDENTITY, bias=bias[:, m : m + 1])
+                    else:
+                        nc.vector.tensor_scalar_add(out=y_part, in0=sums, scalar1=bias[:, m : m + 1])
+                if (m, a) == (O_TILES - 1, UP - 1):
+                    for i in range(DEPTH):
+                        nc.sync.dma_start(out=planes[:, a, i], in_=y[:, i * UP_PLANE : (i + 1) * UP_PLANE])
+                else:
+                    nc.sync.dma_start(out=planes[:, a], in_=y[:].rearrange("p (i f) -> p i f", i=DEPTH))
 
         def crop_z(i, copy):
             cropped = results.tile([P, UP_POSITIONS], F32)
@@ -271,25 +292,32 @@ def tile_upconvcropcat_k_kernel(tc, x, z, W, b, out):
         both = (scalar_copy, vector_copy)
         warm = const.tile([P, 1], F32)
         nc.scalar.activation(out=warm[:], in_=identity[:, 0:1], func=IDENTITY)
-        transpose(0, 0)
+        keep_busy(5)
+        transpose(0, 0, (0,))
+        keep_busy(1)
+        transpose(0, 0, (1,))
+        keep_busy(2)
         group_x(0, 0, scalar_copy)
+        group_x(0, 1, scalar_copy)
         copy_out(0, 0, (vector_copy, scalar_copy))
         quantise(0, 0, first)
         quantise_x(0, 0)
-        group_x(0, 1, scalar_copy)
-        quantise(0, 0, last)
         quantise_x(0, 1)
+        quantise(0, 0, last)
         nc.vector.tensor_copy(out=b_rows_f32[:], in_=b_rows[:])
         multiply(0, 0, first)
         transpose(0, 1)
-        b_turned = turn_bias()
         group_x(0, 2, scalar_copy)
         group_x(0, 3, vector_copy)
         quantise_x(0, 2)
         quantise_x(0, 3)
+        copy_out(0, 1, both)
+        transpose(0, 2)
         multiply(0, 0, last)
+        b_turned = None
         for piece in range(1, PIECES):
-            copy_out(0, piece, both)
+            if piece > 1:
+                copy_out(0, piece, both)
             group_x(piece, 0, vector_copy)
             quantise(0, piece, every)
             for g in every:
@@ -297,10 +325,12 @@ def tile_upconvcropcat_k_kernel(tc, x, z, W, b, out):
                     group_x(piece, g, scalar_copy)
                 quantise_x(piece, g)
             if piece == 1:
+                multiply(0, 1, every)
+                transpose(0, 3)
+                b_turned = turn_bias()
+            if piece == 2:
                 nc.scalar.activation(out=bias[:], in_=b_turned[:, 0:O_TILES], func=IDENTITY)
-            if piece + 1 < PIECES:
-                transpose(0, piece + 1)
-                multiply(0, piece, every)
+                multiply(0, 2, every)
         runs = []
         for m in range(1, O_TILES):
             for piece in range(0, PIECES, 2):

from contextlib import ExitStack

import concourse.mybir as mybir
from concourse.masks import make_identity

F32 = mybir.dt.float32
BF16 = mybir.dt.bfloat16
U32 = mybir.dt.uint32
U8 = mybir.dt.uint8
FP8X4 = mybir.dt.float8_e4m3fn_x4
IDENTITY = mybir.ActivationFunctionType.Identity


P = 128
PACK = 4
K_PASS = P * PACK
PAIR = 2
BANK_WORDS = 512
PSUM_BANKS = 8

CHANNELS = 8192
OUT_CHANNELS = 512
Z_CHANNELS = 512
DEPTH = 2
HEIGHT = 4
WIDTH = 16
POSITIONS = DEPTH * HEIGHT * WIDTH
UP = 2
UP_PLANE = UP * HEIGHT * UP * WIDTH
UP_POSITIONS = UP * DEPTH * UP_PLANE
MARGIN = 2
Z_HEIGHT = UP * HEIGHT + 2 * MARGIN
Z_WIDTH = UP * WIDTH + 2 * MARGIN

PASSES = CHANNELS // K_PASS
O_TILES = OUT_CHANNELS // P
Z_TILES = Z_CHANNELS // P
N_MOVING = UP * POSITIONS
GROUPS = UP * UP

PIECE_PASSES = 4
PIECE_K = PIECE_PASSES * K_PASS
PIECE_WORDS = PIECE_K // PAIR
PIECES = PASSES // PIECE_PASSES
PIECE_BANKS = PIECE_WORDS // BANK_WORDS
BANK_PASSES = PIECE_PASSES // PIECE_BANKS

FLOPS = 2 * OUT_CHANNELS * CHANNELS * UP_POSITIONS
BYTES = (
    2 * (CHANNELS * POSITIONS + OUT_CHANNELS * CHANNELS + OUT_CHANNELS + Z_CHANNELS * UP_POSITIONS)
    + 4 * (OUT_CHANNELS + Z_CHANNELS) * UP_POSITIONS
)


def tile_upconvcropcat_k_kernel(tc, x, z, W, b, out):
    nc = tc.nc
    x_rows = x.rearrange("n c d h w -> (n c) (d h w)")
    z_rows = z.rearrange("n c d h w -> (n c) d (h w)")
    out_rows = out.rearrange("n c d h w -> (n c) (d h w)")

    with ExitStack() as stack:
        const = stack.enter_context(tc.tile_pool(name="const", bufs=1))
        x_raw_pool = stack.enter_context(tc.tile_pool(name="x_raw", bufs=PIECES))
        w_raw_pool = stack.enter_context(tc.tile_pool(name="w_raw", bufs=O_TILES * PIECES))
        z_raw_pool = stack.enter_context(tc.tile_pool(name="z_raw", bufs=Z_TILES))
        x_mx_pool = stack.enter_context(tc.tile_pool(name="x_mx", bufs=PIECES))
        stage = stack.enter_context(tc.tile_pool(name="stage", bufs=4))
        results = stack.enter_context(tc.tile_pool(name="results", bufs=4))
        acc_pool = stack.enter_context(tc.psum_pool(name="acc", bufs=GROUPS))
        turned_pool = stack.enter_context(tc.psum_pool(name="turned", bufs=PSUM_BANKS - GROUPS))
        stack.enter_context(tc.manual_schedule())

        x_raws = []
        w_raws = {}
        z_raws = []

        def load_w(m, piece, passes):
            if passes[0] == 0:
                w_raw = w_raw_pool.tile([P, PIECE_K], BF16)
                w_raws[m, piece] = w_raw
            cols = slice(passes[0] * K_PASS, (passes[-1] + 1) * K_PASS)
            nc.sync.dma_start(
                out=w_raws[m, piece][:, cols],
                in_=W[m * P : (m + 1) * P, piece * PIECE_K + cols.start : piece * PIECE_K + cols.stop],
            )

        def load_x(piece, passes):
            if passes[0] == 0:
                x_raw = x_raw_pool.tile([P, PIECE_K], BF16)
                x_raws.append(x_raw)
            cols = slice(passes[0] * K_PASS, (passes[-1] + 1) * K_PASS)
            first = piece * PIECE_K
            nc.sync.dma_start(
                out=x_raws[piece][:, cols].rearrange("p (g f) -> p g f", f=PACK * POSITIONS),
                in_=x_rows[first + cols.start : first + cols.stop, :].rearrange("(g q t) w -> q g (t w)", q=P, t=PACK),
            )

        def load_z(i):
            z_raw = z_raw_pool.tile([P, UP * DEPTH * Z_HEIGHT * Z_WIDTH], BF16)
            nc.sync.dma_start(
                out=z_raw[:],
                in_=z_rows[i * P : (i + 1) * P, MARGIN : MARGIN + UP * DEPTH, :].rearrange("c d f -> c (d f)"),
            )
            z_raws.append(z_raw)

        first, last, every = (0, 1), (2, 3), (0, 1, 2, 3)
        load_w(0, 0, first)
        load_x(0, first)
        load_w(0, 0, last)
        load_x(0, last)
        load_w(0, 1, every)
        load_w(0, 2, every)
        load_x(1, every)
        load_x(2, every)
        load_w(0, 3, every)
        load_x(3, every)
        for m in range(1, O_TILES):
            for piece in range(PIECES):
                load_w(m, piece, every)
            if m == 1:
                for i in range(Z_TILES):
                    load_z(i)

        vector_copy = nc.vector.tensor_copy
        scalar_copy = nc.scalar.copy
        identity = const.tile([P, P], F32)
        make_identity(nc, identity[:])

        ordered_words = {}

        def order(m, piece, copy):
            w_ordered = stage.tile([P, PIECE_K], BF16, align_bytes=64)
            copy(
                out=w_ordered[:].bitcast(F32).rearrange("p (g u q) -> p g u q", g=PIECE_PASSES, u=PAIR),
                in_=w_raws[m, piece][:].bitcast(F32).rearrange("p (g q u) -> p g u q", g=PIECE_PASSES, u=PAIR),
            )
            ordered_words[m, piece] = w_ordered

        turned_banks = {}

        def transpose(m, piece, halves=(0, 1)):
            banks = turned_banks.setdefault((m, piece), [])
            for h in halves:
                turned = turned_pool.tile([P, BANK_WORDS], F32, tag="turned")
                for s in range(BANK_WORDS // P):
                    if (m, piece) in ordered_words:
                        first_word = h * BANK_WORDS + s * P
                        words = ordered_words[m, piece][:].bitcast(F32)[:, first_word : first_word + P]
                    else:
                        g, u = divmod(s, PAIR)
                        first_word = h * BANK_WORDS + g * PAIR * P
                        words = w_raws[m, piece][:].bitcast(F32)[:, first_word + u : first_word + PAIR * P : PAIR]
                    nc.tensor.transpose(out=turned[:, s * P : (s + 1) * P], in_=words, identity=identity[:])
                banks.append(turned)

        zeros = const.tile([P, BANK_WORDS], BF16)
        nc.vector.memset(zeros[:], 0.0)
        idle_bank = turned_pool.tile([P, BANK_WORDS], F32, tag="turned")

        def keep_busy(count):
            for k in range(count):
                nc.tensor.matmul(out=idle_bank[:], lhsT=zeros[:, 0:P], rhs=zeros[:], start=True, stop=True)

        w_groups = {}

        def copy_out(m, piece, copies):
            w_grouped = stage.tile([P, PIECE_K], BF16, align_bytes=64)
            grouped_words = w_grouped[:].bitcast(F32)
            for h in range(PIECE_BANKS):
                copies[h](
                    out=grouped_words[:, h * BANK_WORDS : (h + 1) * BANK_WORDS].rearrange(
                        "p (g o u) -> p g o u", g=BANK_PASSES, u=PAIR
                    ),
                    in_=turned_banks[m, piece][h][:].rearrange("p (g u o) -> p g o u", g=BANK_PASSES, u=PAIR),
                )
            w_groups[m, piece] = w_grouped

        w_quantised = {}

        def quantise(m, piece, passes):
            if passes[0] == 0:
                w_words = stage.tile([P, PIECE_PASSES * P], U32, bufs=8, align_bytes=64)
                w_scales = stage.tile([P, PIECE_PASSES * P], U8, bufs=8, align_bytes=64)
                w_quantised[m, piece] = (w_words, w_scales)
            w_words, w_scales = w_quantised[m, piece]
            cols = slice(passes[0] * P, (passes[-1] + 1) * P)
            nc.vector.quantize_mx(
                out=w_words[:, cols].bitcast(FP8X4),
                scales=w_scales[:, cols],
                in_=w_groups[m, piece][:, passes[0] * K_PASS : (passes[-1] + 1) * K_PASS],
            )

        x_groups = []
        x_quantised = []

        def group_x(piece, g, copy):
            if g == 0:
                x_grouped = stage.tile([P, PIECE_K], BF16, bufs=3, align_bytes=64)
                x_groups.append(x_grouped)
            cols = slice(g * K_PASS, (g + 1) * K_PASS)
            copy(
                out=x_groups[piece][:, cols].rearrange("p (c i t) -> p c t i", i=4, t=PACK),
                in_=x_raws[piece][:, cols].rearrange("p (t c i) -> p c t i", t=PACK, i=4),
            )

        def quantise_x(piece, g):
            if g == 0:
                x_words = x_mx_pool.tile([P, PIECE_PASSES * N_MOVING], U32, align_bytes=64)
                x_scales = x_mx_pool.tile([P, PIECE_PASSES * N_MOVING], U8, align_bytes=64)
                x_quantised.append((x_words, x_scales))
            x_words, x_scales = x_quantised[piece]
            for r in range(UP):
                cols = slice(g * N_MOVING + r * POSITIONS, g * N_MOVING + (r + 1) * POSITIONS)
                nc.vector.quantize_mx(
                    out=x_words[:, cols].bitcast(FP8X4),
                    scales=x_scales[:, cols],
                    in_=x_groups[piece][:, g * K_PASS : (g + 1) * K_PASS],
                )

        accs = {}

        def multiply(m, piece, passes):
            if piece == 0 and passes[0] == 0:
                accs[m] = []
                for j in range(GROUPS):
                    group = acc_pool.tile([P, N_MOVING], F32)
                    accs[m].append(group)
            w_words, w_scales = w_quantised[m, piece]
            x_words, x_scales = x_quantised[piece]
            steps = [(g, j) for g in passes for j in range(GROUPS)]
            if (m, piece) == (O_TILES - 1, PIECES - 1):
                steps = [(g, j) for j in range(GROUPS) for g in passes]
            for g, j in steps:
                c = piece * PIECE_PASSES + g
                o_cols = slice(g * P, (g + 1) * P)
                x_cols = slice(g * N_MOVING, (g + 1) * N_MOVING)
                nc.tensor.matmul_mx(
                    out=accs[m][j][:],
                    lhsT=w_words[:, o_cols].bitcast(FP8X4),
                    lhsT_scale=w_scales[:, o_cols],
                    rhs=x_words[:, x_cols].bitcast(FP8X4),
                    rhs_scale=x_scales[:, x_cols],
                    start=(c == 0),
                    stop=(c == PASSES - 1),
                )

        def finish(m):
            planes = out_rows[m * P : (m + 1) * P, :].rearrange("o (i a f) -> o a i f", i=DEPTH, a=UP)
            for a in range(UP):
                y = results.tile([P, DEPTH * UP_PLANE], F32)
                y_view = y[:].rearrange("p (i h b k r) -> p b i h k r", i=DEPTH, h=HEIGHT, b=UP, k=WIDTH, r=UP)
                views = []
                for bb in range(UP):
                    sums = accs[m][a * UP + bb][:].rearrange("p (r i h k) -> p i h k r", r=UP, i=DEPTH, h=HEIGHT)
                    if (m, a) == (O_TILES - 1, UP - 1):
                        views.append((y_view[:, bb, 0], sums[:, 0], True))
                        views.append((y_view[:, bb, 1], sums[:, 1], False))
                    else:
                        views.append((y_view[:, bb], sums, bb == 0))
                for y_part, sums, on_scalar in views:
                    if on_scalar:
                        nc.scalar.activation(out=y_part, in_=sums, func=IDENTITY, bias=bias[:, m : m + 1])
                    else:
                        nc.vector.tensor_scalar_add(out=y_part, in0=sums, scalar1=bias[:, m : m + 1])
                if (m, a) == (O_TILES - 1, UP - 1):
                    for i in range(DEPTH):
                        nc.sync.dma_start(out=planes[:, a, i], in_=y[:, i * UP_PLANE : (i + 1) * UP_PLANE])
                else:
                    nc.sync.dma_start(out=planes[:, a], in_=y[:].rearrange("p (i f) -> p i f", i=DEPTH))

        def crop_z(i, copy):
            cropped = results.tile([P, UP_POSITIONS], F32)
            copy(
                out=cropped[:].rearrange("p (d h w) -> p d h w", h=UP * HEIGHT, w=UP * WIDTH),
                in_=z_raws[i][:].rearrange("p (d h w) -> p d h w", h=Z_HEIGHT, w=Z_WIDTH)[
                    :, :, MARGIN : MARGIN + UP * HEIGHT, MARGIN : MARGIN + UP * WIDTH
                ],
            )
            nc.sync.dma_start(out=out_rows[OUT_CHANNELS + i * P : OUT_CHANNELS + (i + 1) * P, :], in_=cropped[:])

        b_rows = const.tile([P, P], BF16)
        nc.vector.memset(b_rows[:], 0.0)
        nc.scalar.dma_start(out=b_rows[0:O_TILES, :], in_=b.rearrange("(m o) -> m o", m=O_TILES))
        b_rows_f32 = const.tile([P, P], F32)
        bias = const.tile([P, O_TILES], F32)

        def turn_bias():
            b_turned = turned_pool.tile([P, BANK_WORDS], F32, tag="turned")
            nc.tensor.transpose(out=b_turned[:, 0:P], in_=b_rows_f32[:], identity=identity[:])
            return b_turned

        both = (scalar_copy, vector_copy)
        warm = const.tile([P, 1], F32)
        nc.scalar.activation(out=warm[:], in_=identity[:, 0:1], func=IDENTITY)
        keep_busy(5)
        transpose(0, 0, (0,))
        keep_busy(1)
        transpose(0, 0, (1,))
        keep_busy(2)
        group_x(0, 0, scalar_copy)
        group_x(0, 1, scalar_copy)
        copy_out(0, 0, (vector_copy, scalar_copy))
        quantise(0, 0, first)
        quantise_x(0, 0)
        quantise_x(0, 1)
        quantise(0, 0, last)
        nc.vector.tensor_copy(out=b_rows_f32[:], in_=b_rows[:])
        multiply(0, 0, first)
        transpose(0, 1)
        group_x(0, 2, scalar_copy)
        group_x(0, 3, vector_copy)
        quantise_x(0, 2)
        quantise_x(0, 3)
        copy_out(0, 1, both)
        transpose(0, 2)
        multiply(0, 0, last)
        b_turned = None
        for piece in range(1, PIECES):
            if piece > 1:
                copy_out(0, piece, both)
            group_x(piece, 0, vector_copy)
            quantise(0, piece, every)
            for g in every:
                if g > 0:
                    group_x(piece, g, scalar_copy)
                quantise_x(piece, g)
            if piece == 1:
                multiply(0, 1, every)
                transpose(0, 3)
                b_turned = turn_bias()
            if piece == 2:
                nc.scalar.activation(out=bias[:], in_=b_turned[:, 0:O_TILES], func=IDENTITY)
                multiply(0, 2, every)
        runs = []
        for m in range(1, O_TILES):
            for piece in range(0, PIECES, 2):
                runs.append(((m, piece), (m, piece + 1)))
        waiting = [(0, PIECES - 1)]
        for j, run in enumerate(runs):
            for step in run:
                transpose(*step)
            for step in run:
                copy_out(*step, both)
            if j + 1 < len(runs):
                for step in runs[j + 1]:
                    order(*step, scalar_copy)
            for step in run:
                quantise(*step, every)
            for step in waiting:
                multiply(*step, every)
                if step[1] == PIECES - 1:
                    finish(step[0])
            if j in (1, 2, 3, 4):
                crop_z(j - 1, vector_copy)
            waiting = run
        for step in waiting:
            multiply(*step, every)
        finish(O_TILES - 1)
